import numpy as np
import ml_dtypes


def mxq(x, axis, fmt="e4m3"):
    dtype, down = {"e4m3": (ml_dtypes.float8_e4m3fn, 7), "e5m2": (ml_dtypes.float8_e5m2, 14)}[fmt]
    v = np.moveaxis(np.asarray(x, np.float32).astype(ml_dtypes.bfloat16).astype(np.float64), axis, -1)
    blocks = v.reshape(v.shape[:-1] + (-1, 32))
    amax = np.abs(blocks).max(-1, keepdims=True)
    byte = np.maximum(np.where(amax > 0, np.frexp(amax)[1] - 1 + 127, 0) - down, 1)
    scale = np.exp2(byte - 127.0)
    codes = (blocks / scale).astype(np.float32).astype(dtype).astype(np.float64)
    return np.moveaxis((codes * scale).reshape(v.shape), -1, axis)


WIDE = False


def mx_kscale(k):
    if not WIDE:
        return np.ones(k)
    levels = np.array([10, -10, 5, -5, 0])
    if k % 512:
        return np.exp2(np.random.permutation(np.resize(levels, k // 32))).repeat(32)
    a = np.empty((k // 512, 16))
    for p in range(k // 512):
        a[p, :8] = np.random.permutation(np.resize(levels, 8))
        for g in range(8):
            far = levels[np.abs(levels - a[p, g]) >= 10]
            a[p, g + 8] = far[np.random.randint(len(far))]
    return np.exp2(a.ravel()).repeat(32)


BF16 = ml_dtypes.bfloat16


def bf(x):
    return np.asarray(x, np.float32).astype(BF16)


def f64(x):
    return np.asarray(x).astype(np.float64)


N, IN_DIM, HID, OUT_DIM = 1024, 1024, 512, 256
CAT = 3 * HID


def log_softmax(v):
    d = v - v.max(-1, keepdims=True)
    return d - np.log(np.exp(d).sum(-1, keepdims=True))


def setup_inputs():
    s, t = mx_kscale(HID), mx_kscale(CAT)
    ta, tb, tc = t[:HID], t[HID:2 * HID], t[2 * HID:]
    return {"u1": bf(np.maximum(np.random.standard_normal((N, HID)) * 2.0, 0.0) * s),
            "W2_1": bf(np.random.standard_normal((HID, HID)) * 0.5 / np.sqrt(HID) / s[:, None] * tc),
            "b2_1": bf(np.random.standard_normal(HID) * 0.3 * tc),
            "h": bf(np.random.standard_normal((N, HID)) * ta),
            "h1": bf(np.random.standard_normal((N, HID)) * 0.8 * tb),
            "W_out": bf(np.random.standard_normal((CAT, OUT_DIM)) * 2.0 / np.sqrt(CAT) / t[:, None]),
            "b_out": bf(np.random.standard_normal(OUT_DIM) * 0.3)}


def reference(u1, W2_1, b2_1, h, h1, W_out, b_out):
    h2 = (mxq(f64(u1), 1, "e4m3") @ mxq(f64(W2_1), 0, "e4m3")) + f64(b2_1)
    cat = np.concatenate([f64(h), f64(h1), h2], axis=-1)
    logits = (mxq(cat, 1, "e4m3") @ mxq(f64(W_out), 0, "e4m3")) + f64(b_out)
    return log_softmax(logits)

@@ -1,0 +1,280 @@
+from contextlib import ExitStack
+
+import concourse.mybir as mybir
+from concourse.masks import make_identity
+
+F32 = mybir.dt.float32
+BF16 = mybir.dt.bfloat16
+U32 = mybir.dt.uint32
+U8 = mybir.dt.uint8
+FP8X4 = mybir.dt.float8_e4m3fn_x4
+ALU = mybir.AluOpType
+ACT = mybir.ActivationFunctionType
+AX = mybir.AxisListType
+
+P = 128
+NODES = 1024
+HID = 512
+CLASSES = 256
+TILES = NODES // P
+PAIRS = TILES // 2
+WORDS = HID // 2
+FLOPS = 2 * NODES * HID * HID + 2 * NODES * 3 * HID * CLASSES
+
+
+def tile_gin_pc_kernel(tc, u1, W2_1, b2_1, h, h1, W_out, b_out, out):
+    nc = tc.nc
+    with ExitStack() as ctx:
+        keep = ctx.enter_context(tc.tile_pool(name="keep", bufs=1))
+        psum = ctx.enter_context(tc.psum_pool(name="psum", bufs=7))
+        ctx.enter_context(tc.manual_schedule())
+
+        ident = keep.tile([P, P], F32)
+        make_identity(nc, ident[:])
+        ones = keep.tile([P, P], BF16)
+        nc.gpsimd.memset(ones[:], 1.0)
+        bo_rows = keep.tile([P, CLASSES], BF16)
+        nc.vector.memset(bo_rows[:], 0.0)
+        warm_rhs = keep.tile([P, CLASSES], F32)
+        nc.vector.memset(warm_rhs[:], 0.0)
+        warm_out = psum.tile([P, CLASSES], F32, tag="warm", bufs=1)
+
+        def keep_warm(times):
+            for rep in range(times):
+                nc.tensor.matmul(out=warm_out[:], lhsT=ident[:], rhs=warm_rhs[:], start=True, stop=True)
+
+        keep_warm(2)
+
+        w2_raw = keep.tile([P, 4 * HID], BF16)
+        u1_sb = keep.tile([P, TILES * HID], BF16)
+        h_sb = keep.tile([P, TILES * HID], BF16)
+        h1_sb = keep.tile([P, TILES * HID], BF16)
+        wo_raw = keep.tile([P, 12 * CLASSES], BF16)
+        b2_raw = keep.tile([P, 4], BF16)
+
+        def load_tiles(x_sb, x, lo, hi):
+            cols = slice(lo * HID, hi * HID)
+            nc.sync.dma_start(out=x_sb[:, cols], in_=x.rearrange("(p i) k -> p (i k)", i=TILES)[:, cols])
+
+        nc.scalar.dma_start(out=b2_raw[:], in_=b2_1.rearrange("(p t) -> p t", t=4))
+        nc.scalar.dma_start(out=bo_rows[0:1, :], in_=b_out.rearrange("(o c) -> o c", o=1))
+        nc.sync.dma_start(
+            out=w2_raw[:],
+            in_=W2_1.rearrange("(q t) c -> q (t c)", t=4),
+        )
+        load_tiles(u1_sb, u1, 0, 2)
+        load_tiles(u1_sb, u1, 2, 4)
+        load_tiles(u1_sb, u1, 4, 8)
+        nc.sync.dma_start(
+            out=wo_raw[:, 0 : 8 * CLASSES].rearrange("q (g x) -> q g x", g=2),
+            in_=W_out[0 : 2 * HID, :].rearrange("(g q t) c -> q g (t c)", g=2, t=4),
+        )
+        nc.sync.dma_start(
+            out=wo_raw[:, 8 * CLASSES : 12 * CLASSES],
+            in_=W_out[2 * HID : 3 * HID, :].rearrange("(q t) c -> q (t c)", t=4),
+        )
+        load_tiles(h_sb, h, 0, 4)
+        load_tiles(h1_sb, h1, 0, 4)
+        load_tiles(h_sb, h, 4, 8)
+        load_tiles(h1_sb, h1, 4, 8)
+
+        w2_g = keep.tile([P, 4 * HID], BF16, align_bytes=64)
+        w2_c = keep.tile([P, HID], U32, align_bytes=64)
+        w2_s = keep.tile([P, HID], U8, align_bytes=64)
+        wo_g = keep.tile([P, 12 * CLASSES], BF16, align_bytes=64)
+        wo_c = keep.tile([P, 3 * CLASSES], U32, align_bytes=64)
+        wo_s = keep.tile([P, 3 * CLASSES], U8, align_bytes=64)
+        u1_g = keep.tile([P, TILES * HID], BF16, align_bytes=64)
+        u1_c = keep.tile([P, NODES], U32, align_bytes=64)
+        u1_s = keep.tile([P, NODES], U8, align_bytes=64)
+        h_g = keep.tile([P, TILES * HID], BF16, align_bytes=64)
+        h_c = keep.tile([P, NODES], U32, align_bytes=64)
+        h_s = keep.tile([P, NODES], U8, align_bytes=64)
+        h1_g = keep.tile([P, TILES * HID], BF16, align_bytes=64)
+        h1_c = keep.tile([P, NODES], U32, align_bytes=64)
+        h1_s = keep.tile([P, NODES], U8, align_bytes=64)
+        h2_g = keep.tile([P, TILES * HID], BF16, align_bytes=64)
+        h2_c = keep.tile([P, NODES], U32, align_bytes=64)
+        h2_s = keep.tile([P, NODES], U8, align_bytes=64)
+        bo = keep.tile([P, CLASSES], F32)
+        z = keep.tile([P, TILES * CLASSES], F32)
+        junk = keep.tile([P, CLASSES], F32)
+        negm = keep.tile([P, TILES], F32)
+        ssum = keep.tile([P, TILES], F32)
+        lse = keep.tile([P, TILES], F32)
+
+        def quantise(g, c, s, lo, hi):
+            nc.vector.quantize_mx(out=c[:, lo:hi].bitcast(FP8X4), scales=s[:, lo:hi], in_=g[:, 4 * lo : 4 * hi])
+
+        def transposes(x_sb, pair):
+            tp = psum.tile([P, 2, 2, P], F32, tag="bank")
+            words = x_sb[:].bitcast(F32)
+            for s in range(2):
+                for u in range(2):
+                    col = (2 * pair + s) * WORDS
+                    nc.tensor.transpose(tp[:, s, u, :], words[:, col + u : col + WORDS : 2], ident[:])
+            return tp
+
+        def copy_out(engine_copy, tp, g, pair):
+            dst = g[:].bitcast(F32)[:, 2 * pair * WORDS : (2 * pair + 2) * WORDS]
+            engine_copy(
+                out=dst.rearrange("p (s n u) -> p s n u", s=2, u=2),
+                in_=tp[:].rearrange("p s u n -> p s n u"),
+            )
+
+        def stage1_mm(i):
+            hp = psum.tile([P, 4, P], F32, tag="bank")
+            for t in range(4):
+                nc.tensor.matmul_mx(
+                    out=hp[:, t, :],
+                    lhsT=w2_c[:, t * P : (t + 1) * P].bitcast(FP8X4),
+                    lhsT_scale=w2_s[:, t * P : (t + 1) * P],
+                    rhs=u1_c[:, i * P : (i + 1) * P].bitcast(FP8X4),
+                    rhs_scale=u1_s[:, i * P : (i + 1) * P],
+                    start=True,
+                    stop=True,
+                )
+            return hp
+
+        def stage1_out(hp, i):
+            nc.vector.tensor_tensor(
+                out=h2_g[:, i * HID : (i + 1) * HID].rearrange("p (n t) -> p n t", t=4),
+                in0=hp[:].rearrange("p t n -> p n t"),
+                in1=b2_raw[:].unsqueeze(1).to_broadcast([P, P, 4]),
+                op=ALU.add,
+            )
+
+        def stage1_out_scalar(hp, i):
+            dst = h2_g[:, i * HID : (i + 1) * HID].rearrange("p (n t) -> p n t", t=4)
+            for t in range(4):
+                nc.scalar.activation(
+                    out=dst[:, :, t], in_=hp[:, t, :], func=ACT.Identity, bias=b2_raw[:, t : t + 1], scale=1.0
+                )
+
+        def stage2_mm(pair):
+            lp = psum.tile([P, 2, CLASSES], F32, tag="bank")
+            for s in range(2):
+                i = 2 * pair + s
+                for g, (c, sc) in enumerate(((h_c, h_s), (h1_c, h1_s), (h2_c, h2_s))):
+                    nc.tensor.matmul_mx(
+                        out=lp[:, s, :],
+                        lhsT=c[:, i * P : (i + 1) * P].bitcast(FP8X4),
+                        lhsT_scale=sc[:, i * P : (i + 1) * P],
+                        rhs=wo_c[:, g * CLASSES : (g + 1) * CLASSES].bitcast(FP8X4),
+                        rhs_scale=wo_s[:, g * CLASSES : (g + 1) * CLASSES],
+                        start=(g == 0),
+                        stop=(g == 2),
+                    )
+            return lp
+
+        def logits_max(lp, pair):
+            zp = z[:, 2 * pair * CLASSES : (2 * pair + 2) * CLASSES].rearrange("p (s c) -> p s c", s=2)
+            nc.vector.tensor_tensor(
+                out=zp, in0=lp[:], in1=bo[:].unsqueeze(1).to_broadcast([P, 2, CLASSES]), op=ALU.add
+            )
+            nc.vector.tensor_reduce(
+                out=negm[:, 2 * pair : 2 * pair + 2], in_=zp, axis=AX.X, op=ALU.max, negate=True
+            )
+
+        def exps(pair):
+            for i in (2 * pair, 2 * pair + 1):
+                nc.scalar.activation(
+                    out=junk[:],
+                    in_=z[:, i * CLASSES : (i + 1) * CLASSES],
+                    func=ACT.Exp,
+                    bias=negm[:, i : i + 1],
+                    scale=1.0,
+                    accum_out=ssum[:, i : i + 1],
+                )
+
+        w2_dst = w2_g[:].rearrange("p (t2 p2 t) -> p t2 p2 t", t2=4, t=4)
+        w2_src = w2_raw[:].rearrange("p (t p2 t2) -> p t2 p2 t", t=4, t2=4)
+        nc.vector.tensor_copy(out=w2_dst[:, 0:3], in_=w2_src[:, 0:3])
+        nc.scalar.copy(out=w2_dst[:, 3], in_=w2_src[:, 3])
+        quantise(w2_g, w2_c, w2_s, 0, HID)
+
+        def regroup_wo(g):
+            cols = slice(g * 4 * CLASSES, (g + 1) * 4 * CLASSES)
+            nc.gpsimd.tensor_scalar(
+                out=wo_g[:, cols].rearrange("p (c t) -> p c t", t=4),
+                in0=wo_raw[:, cols].rearrange("p (t c) -> p c t", t=4),
+                scalar1=1.0,
+                scalar2=0.0,
+                op0=ALU.mult,
+                op1=ALU.add,
+            )
+
+        u1_tp = [transposes(u1_sb, 0), transposes(u1_sb, 1)]
+        bp = psum.tile([P, CLASSES], F32, tag="bank")
+        nc.tensor.matmul(out=bp[:], lhsT=ones[:], rhs=bo_rows[:], start=True, stop=True)
+        keep_warm(1)
+        u1_tp.append(transposes(u1_sb, 2))
+        u1_tp.append(transposes(u1_sb, 3))
+        copy_out(nc.scalar.copy, u1_tp[0], u1_g, 0)
+        quantise(u1_g, u1_c, u1_s, 0, 2 * P)
+        copy_out(nc.scalar.copy, u1_tp[1], u1_g, 1)
+        quantise(u1_g, u1_c, u1_s, 2 * P, 4 * P)
+        copy_out(nc.scalar.copy, u1_tp[2], u1_g, 2)
+        copy_out(nc.scalar.copy, u1_tp[3], u1_g, 3)
+        nc.scalar.copy(out=bo[:], in_=bp[:])
+        hps = [stage1_mm(i) for i in range(4)]
+        keep_warm(1)
+        stage1_out(hps[0], 0)
+        quantise(u1_g, u1_c, u1_s, 4 * P, 8 * P)
+        stage1_out(hps[1], 1)
+        for i in range(4, TILES):
+            hps.append(stage1_mm(i))
+        keep_warm(1)
+        for g in range(3):
+            regroup_wo(g)
+        stage1_out_scalar(hps[2], 2)
+        stage1_out_scalar(hps[6], 6)
+        for i in (3, 4, 5, 7):
+            stage1_out(hps[i], i)
+        quantise(h2_g, h2_c, h2_s, 0, 4 * P)
+
+        x_tp = {}
+        for pair in range(PAIRS):
+            x_tp[(0, pair)] = transposes(h_sb, pair)
+            x_tp[(1, pair)] = transposes(h1_sb, pair)
+            if pair % 2 == 1:
+                keep_warm((pair + 1) // 2)
+        for pair in range(PAIRS):
+            copy_out(nc.scalar.copy, x_tp[(0, pair)], h_g, pair)
+            copy_out(nc.scalar.copy, x_tp[(1, pair)], h1_g, pair)
+        quantise(wo_g, wo_c, wo_s, 0, 2 * CLASSES)
+        quantise(h2_g, h2_c, h2_s, 4 * P, 8 * P)
+        quantise(wo_g, wo_c, wo_s, 2 * CLASSES, 3 * CLASSES)
+
+        def quantise_pair(pair):
+            quantise(h_g, h_c, h_s, 2 * pair * P, (2 * pair + 2) * P)
+            quantise(h1_g, h1_c, h1_s, 2 * pair * P, (2 * pair + 2) * P)
+
+        lps = []
+        for pair in range(3):
+            quantise_pair(pair)
+            lps.append(stage2_mm(pair))
+            if pair == 1:
+                keep_warm(1)
+        logits_max(lps[0], 0)
+        exps(0)
+        quantise_pair(3)
+        lps.append(stage2_mm(3))
+        for pair in range(1, PAIRS):
+            logits_max(lps[pair], pair)
+            exps(pair)
+        nc.scalar.activation(out=lse[:], in_=ssum[:], func=ACT.Ln)
+        out_rows = out.rearrange("(p i) c -> p (i c)", i=TILES)
+        for pair in range(PAIRS):
+            for i in (2 * pair, 2 * pair + 1):
+                zi = z[:, i * CLASSES : (i + 1) * CLASSES]
+                nc.vector.tensor_scalar(
+                    out=zi,
+                    in0=zi,
+                    scalar1=negm[:, i : i + 1],
+                    scalar2=lse[:, i : i + 1],
+                    op0=ALU.add,
+                    op1=ALU.subtract,
+                )
+            cols = slice(2 * pair * CLASSES, (2 * pair + 2) * CLASSES)
+            nc.sync.dma_start(out=out_rows[:, cols], in_=z[:, cols])

@@ -26,7 +26,7 @@ def tile_gin_pc_kernel(tc, u1, W2_1, b2_1, h, h1, W_out, b_out, out):
     nc = tc.nc
     with ExitStack() as ctx:
         keep = ctx.enter_context(tc.tile_pool(name="keep", bufs=1))
-        psum = ctx.enter_context(tc.psum_pool(name="psum", bufs=7))
+        psum = ctx.enter_context(tc.psum_pool(name="psum", bufs=8))
         ctx.enter_context(tc.manual_schedule())
 
         ident = keep.tile([P, P], F32)
@@ -37,13 +37,9 @@ def tile_gin_pc_kernel(tc, u1, W2_1, b2_1, h, h1, W_out, b_out, out):
         nc.vector.memset(bo_rows[:], 0.0)
         warm_rhs = keep.tile([P, CLASSES], F32)
         nc.vector.memset(warm_rhs[:], 0.0)
-        warm_out = psum.tile([P, CLASSES], F32, tag="warm", bufs=1)
-
-        def keep_warm(times):
-            for rep in range(times):
-                nc.tensor.matmul(out=warm_out[:], lhsT=ident[:], rhs=warm_rhs[:], start=True, stop=True)
-
-        keep_warm(2)
+        warm_out = psum.tile([P, CLASSES], F32, tag="bank")
+        for rep in range(2):
+            nc.tensor.matmul(out=warm_out[:], lhsT=ident[:], rhs=warm_rhs[:], start=True, stop=True)
 
         w2_raw = keep.tile([P, 4 * HID], BF16)
         u1_sb = keep.tile([P, TILES * HID], BF16)
@@ -69,12 +65,12 @@ def tile_gin_pc_kernel(tc, u1, W2_1, b2_1, h, h1, W_out, b_out, out):
             out=wo_raw[:, 0 : 8 * CLASSES].rearrange("q (g x) -> q g x", g=2),
             in_=W_out[0 : 2 * HID, :].rearrange("(g q t) c -> q g (t c)", g=2, t=4),
         )
+        load_tiles(h_sb, h, 0, 4)
+        load_tiles(h1_sb, h1, 0, 4)
         nc.sync.dma_start(
             out=wo_raw[:, 8 * CLASSES : 12 * CLASSES],
             in_=W_out[2 * HID : 3 * HID, :].rearrange("(q t) c -> q (t c)", t=4),
         )
-        load_tiles(h_sb, h, 0, 4)
-        load_tiles(h1_sb, h1, 0, 4)
         load_tiles(h_sb, h, 4, 8)
         load_tiles(h1_sb, h1, 4, 8)
 
@@ -189,9 +185,8 @@ def tile_gin_pc_kernel(tc, u1, W2_1, b2_1, h, h1, W_out, b_out, out):
 
         w2_dst = w2_g[:].rearrange("p (t2 p2 t) -> p t2 p2 t", t2=4, t=4)
         w2_src = w2_raw[:].rearrange("p (t p2 t2) -> p t2 p2 t", t=4, t2=4)
-        nc.vector.tensor_copy(out=w2_dst[:, 0:3], in_=w2_src[:, 0:3])
-        nc.scalar.copy(out=w2_dst[:, 3], in_=w2_src[:, 3])
-        quantise(w2_g, w2_c, w2_s, 0, HID)
+        nc.vector.tensor_copy(out=w2_dst[:, 0:2], in_=w2_src[:, 0:2])
+        nc.scalar.copy(out=w2_dst[:, 2:4], in_=w2_src[:, 2:4])
 
         def regroup_wo(g):
             cols = slice(g * 4 * CLASSES, (g + 1) * 4 * CLASSES)
@@ -204,63 +199,89 @@ def tile_gin_pc_kernel(tc, u1, W2_1, b2_1, h, h1, W_out, b_out, out):
                 op1=ALU.add,
             )
 
-        u1_tp = [transposes(u1_sb, 0), transposes(u1_sb, 1)]
+        scopy = nc.scalar.copy
+        vcopy = nc.vector.tensor_copy
+        tp = {}
+        hps = {}
+        lps = {}
+
+        def trans(name, pair):
+            tp[(name, pair)] = transposes({"u": u1_sb, "h": h_sb, "g": h1_sb}[name], pair)
+
+        def copy(engine_copy, name, pair):
+            copy_out(engine_copy, tp[(name, pair)], {"u": u1_g, "h": h_g, "g": h1_g}[name], pair)
+
+        def quant(name, lo_pair, hi_pair):
+            g, c, s = {"u": (u1_g, u1_c, u1_s), "h": (h_g, h_c, h_s), "g": (h1_g, h1_c, h1_s), "2": (h2_g, h2_c, h2_s)}[name]
+            quantise(g, c, s, 2 * lo_pair * P, 2 * hi_pair * P)
+
+        trans("u", 0)
+        trans("u", 1)
+        quantise(w2_g, w2_c, w2_s, 0, HID)
+        trans("u", 2)
+        trans("u", 3)
+        copy(scopy, "u", 0)
+        copy(vcopy, "u", 1)
+        quant("u", 0, 1)
+        copy(scopy, "u", 2)
+        quant("u", 1, 2)
+        copy(scopy, "u", 3)
+        regroup_wo(0)
+        regroup_wo(1)
+        for i in range(4):
+            hps[i] = stage1_mm(i)
+        trans("h", 0)
+        trans("h", 1)
+        stage1_out(hps[0], 0)
+        stage1_out_scalar(hps[1], 1)
+        quant("u", 2, 4)
+        stage1_out(hps[2], 2)
+        stage1_out(hps[3], 3)
+        copy(scopy, "h", 0)
+        for i in range(4, 8):
+            hps[i] = stage1_mm(i)
         bp = psum.tile([P, CLASSES], F32, tag="bank")
         nc.tensor.matmul(out=bp[:], lhsT=ones[:], rhs=bo_rows[:], start=True, stop=True)
-        keep_warm(1)
-        u1_tp.append(transposes(u1_sb, 2))
-        u1_tp.append(transposes(u1_sb, 3))
-        copy_out(nc.scalar.copy, u1_tp[0], u1_g, 0)
-        quantise(u1_g, u1_c, u1_s, 0, 2 * P)
-        copy_out(nc.scalar.copy, u1_tp[1], u1_g, 1)
-        quantise(u1_g, u1_c, u1_s, 2 * P, 4 * P)
-        copy_out(nc.scalar.copy, u1_tp[2], u1_g, 2)
-        copy_out(nc.scalar.copy, u1_tp[3], u1_g, 3)
+        trans("g", 0)
+        trans("g", 1)
+        stage1_out(hps[4], 4)
+        copy(scopy, "h", 1)
+        stage1_out_scalar(hps[5], 5)
         nc.scalar.copy(out=bo[:], in_=bp[:])
-        hps = [stage1_mm(i) for i in range(4)]
-        keep_warm(1)
-        stage1_out(hps[0], 0)
-        quantise(u1_g, u1_c, u1_s, 4 * P, 8 * P)
-        stage1_out(hps[1], 1)
-        for i in range(4, TILES):
-            hps.append(stage1_mm(i))
-        keep_warm(1)
-        for g in range(3):
-            regroup_wo(g)
-        stage1_out_scalar(hps[2], 2)
-        stage1_out_scalar(hps[6], 6)
-        for i in (3, 4, 5, 7):
-            stage1_out(hps[i], i)
-        quantise(h2_g, h2_c, h2_s, 0, 4 * P)
-
-        x_tp = {}
-        for pair in range(PAIRS):
-            x_tp[(0, pair)] = transposes(h_sb, pair)
-            x_tp[(1, pair)] = transposes(h1_sb, pair)
-            if pair % 2 == 1:
-                keep_warm((pair + 1) // 2)
-        for pair in range(PAIRS):
-            copy_out(nc.scalar.copy, x_tp[(0, pair)], h_g, pair)
-            copy_out(nc.scalar.copy, x_tp[(1, pair)], h1_g, pair)
+        stage1_out(hps[6], 6)
+        stage1_out(hps[7], 7)
+        regroup_wo(2)
+        quant("2", 0, 2)
+        copy(scopy, "g", 0)
+        copy(scopy, "g", 1)
+        quant("h", 0, 1)
+        quant("h", 1, 2)
+        trans("h", 2)
+        trans("g", 2)
+        copy(scopy, "h", 2)
         quantise(wo_g, wo_c, wo_s, 0, 2 * CLASSES)
-        quantise(h2_g, h2_c, h2_s, 4 * P, 8 * P)
+        quant("g", 0, 1)
         quantise(wo_g, wo_c, wo_s, 2 * CLASSES, 3 * CLASSES)
-
-        def quantise_pair(pair):
-            quantise(h_g, h_c, h_s, 2 * pair * P, (2 * pair + 2) * P)
-            quantise(h1_g, h1_c, h1_s, 2 * pair * P, (2 * pair + 2) * P)
-
-        lps = []
-        for pair in range(3):
-            quantise_pair(pair)
-            lps.append(stage2_mm(pair))
-            if pair == 1:
-                keep_warm(1)
+        quant("2", 2, 4)
+        quant("g", 1, 2)
+        lps[0] = stage2_mm(0)
+        trans("h", 3)
+        trans("g", 3)
+        lps[1] = stage2_mm(1)
+        copy(scopy, "g", 2)
+        copy(scopy, "h", 3)
+        copy(scopy, "g", 3)
+        quant("h", 2, 3)
         logits_max(lps[0], 0)
         exps(0)
-        quantise_pair(3)
-        lps.append(stage2_mm(3))
-        for pair in range(1, PAIRS):
+        quant("g", 2, 3)
+        lps[2] = stage2_mm(2)
+        quant("h", 3, 4)
+        logits_max(lps[1], 1)
+        exps(1)
+        quant("g", 3, 4)
+        lps[3] = stage2_mm(3)
+        for pair in range(2, PAIRS):
             logits_max(lps[pair], pair)
             exps(pair)
         nc.scalar.activation(out=lse[:], in_=ssum[:], func=ACT.Ln)

@@ -38,8 +38,12 @@ def tile_gin_pc_kernel(tc, u1, W2_1, b2_1, h, h1, W_out, b_out, out):
         warm_rhs = keep.tile([P, CLASSES], F32)
         nc.vector.memset(warm_rhs[:], 0.0)
         warm_out = psum.tile([P, CLASSES], F32, tag="bank")
-        for rep in range(2):
-            nc.tensor.matmul(out=warm_out[:], lhsT=ident[:], rhs=warm_rhs[:], start=True, stop=True)
+
+        def keep_warm(out, times):
+            for rep in range(times):
+                nc.tensor.matmul(out=out, lhsT=ident[:], rhs=warm_rhs[:], start=True, stop=True)
+
+        keep_warm(warm_out[:], 4)
 
         w2_raw = keep.tile([P, 4 * HID], BF16)
         u1_sb = keep.tile([P, TILES * HID], BF16)
@@ -60,7 +64,8 @@ def tile_gin_pc_kernel(tc, u1, W2_1, b2_1, h, h1, W_out, b_out, out):
         )
         load_tiles(u1_sb, u1, 0, 2)
         load_tiles(u1_sb, u1, 2, 4)
-        load_tiles(u1_sb, u1, 4, 8)
+        load_tiles(u1_sb, u1, 4, 6)
+        load_tiles(u1_sb, u1, 6, 8)
         nc.sync.dma_start(
             out=wo_raw[:, 0 : 8 * CLASSES].rearrange("q (g x) -> q g x", g=2),
             in_=W_out[0 : 2 * HID, :].rearrange("(g q t) c -> q g (t c)", g=2, t=4),
@@ -102,8 +107,9 @@ def tile_gin_pc_kernel(tc, u1, W2_1, b2_1, h, h1, W_out, b_out, out):
         def quantise(g, c, s, lo, hi):
             nc.vector.quantize_mx(out=c[:, lo:hi].bitcast(FP8X4), scales=s[:, lo:hi], in_=g[:, 4 * lo : 4 * hi])
 
-        def transposes(x_sb, pair):
+        def transposes(x_sb, pair, warm):
             tp = psum.tile([P, 2, 2, P], F32, tag="bank")
+            keep_warm(tp[:, 0, :, :], warm)
             words = x_sb[:].bitcast(F32)
             for s in range(2):
                 for u in range(2):
@@ -147,8 +153,9 @@ def tile_gin_pc_kernel(tc, u1, W2_1, b2_1, h, h1, W_out, b_out, out):
                     out=dst[:, :, t], in_=hp[:, t, :], func=ACT.Identity, bias=b2_raw[:, t : t + 1], scale=1.0
                 )
 
-        def stage2_mm(pair):
+        def stage2_mm(pair, warm=0):
             lp = psum.tile([P, 2, CLASSES], F32, tag="bank")
+            keep_warm(lp[:, 0, :], warm)
             for s in range(2):
                 i = 2 * pair + s
                 for g, (c, sc) in enumerate(((h_c, h_s), (h1_c, h1_s), (h2_c, h2_s))):
@@ -163,11 +170,14 @@ def tile_gin_pc_kernel(tc, u1, W2_1, b2_1, h, h1, W_out, b_out, out):
                     )
             return lp
 
-        def logits_max(lp, pair):
+        def logits_add(lp, pair):
             zp = z[:, 2 * pair * CLASSES : (2 * pair + 2) * CLASSES].rearrange("p (s c) -> p s c", s=2)
             nc.vector.tensor_tensor(
                 out=zp, in0=lp[:], in1=bo[:].unsqueeze(1).to_broadcast([P, 2, CLASSES]), op=ALU.add
             )
+
+        def logits_max(pair):
+            zp = z[:, 2 * pair * CLASSES : (2 * pair + 2) * CLASSES].rearrange("p (s c) -> p s c", s=2)
             nc.vector.tensor_reduce(
                 out=negm[:, 2 * pair : 2 * pair + 2], in_=zp, axis=AX.X, op=ALU.max, negate=True
             )
@@ -205,8 +215,8 @@ def tile_gin_pc_kernel(tc, u1, W2_1, b2_1, h, h1, W_out, b_out, out):
         hps = {}
         lps = {}
 
-        def trans(name, pair):
-            tp[(name, pair)] = transposes({"u": u1_sb, "h": h_sb, "g": h1_sb}[name], pair)
+        def trans(name, pair, warm=0):
+            tp[(name, pair)] = transposes({"u": u1_sb, "h": h_sb, "g": h1_sb}[name], pair, warm)
 
         def copy(engine_copy, name, pair):
             copy_out(engine_copy, tp[(name, pair)], {"u": u1_g, "h": h_g, "g": h1_g}[name], pair)
@@ -218,7 +228,7 @@ def tile_gin_pc_kernel(tc, u1, W2_1, b2_1, h, h1, W_out, b_out, out):
         trans("u", 0)
         trans("u", 1)
         quantise(w2_g, w2_c, w2_s, 0, HID)
-        trans("u", 2)
+        trans("u", 2, warm=1)
         trans("u", 3)
         copy(scopy, "u", 0)
         copy(vcopy, "u", 1)
@@ -240,49 +250,52 @@ def tile_gin_pc_kernel(tc, u1, W2_1, b2_1, h, h1, W_out, b_out, out):
         copy(scopy, "h", 0)
         for i in range(4, 8):
             hps[i] = stage1_mm(i)
+        copy(scopy, "h", 1)
         bp = psum.tile([P, CLASSES], F32, tag="bank")
         nc.tensor.matmul(out=bp[:], lhsT=ones[:], rhs=bo_rows[:], start=True, stop=True)
         trans("g", 0)
         trans("g", 1)
+        trans("h", 2)
         stage1_out(hps[4], 4)
-        copy(scopy, "h", 1)
         stage1_out_scalar(hps[5], 5)
         nc.scalar.copy(out=bo[:], in_=bp[:])
         stage1_out(hps[6], 6)
         stage1_out(hps[7], 7)
         regroup_wo(2)
         quant("2", 0, 2)
-        copy(scopy, "g", 0)
-        copy(scopy, "g", 1)
-        quant("h", 0, 1)
-        quant("h", 1, 2)
-        trans("h", 2)
-        trans("g", 2)
-        copy(scopy, "h", 2)
-        quantise(wo_g, wo_c, wo_s, 0, 2 * CLASSES)
-        quant("g", 0, 1)
-        quantise(wo_g, wo_c, wo_s, 2 * CLASSES, 3 * CLASSES)
-        quant("2", 2, 4)
-        quant("g", 1, 2)
-        lps[0] = stage2_mm(0)
+        trans("g", 2, warm=1)
         trans("h", 3)
         trans("g", 3)
-        lps[1] = stage2_mm(1)
+        copy(scopy, "g", 0)
+        copy(scopy, "g", 1)
+        quantise(wo_g, wo_c, wo_s, 0, 2 * CLASSES)
+        quant("h", 0, 1)
+        quant("g", 0, 1)
+        quantise(wo_g, wo_c, wo_s, 2 * CLASSES, 3 * CLASSES)
+        lps[0] = stage2_mm(0)
+        copy(scopy, "h", 2)
+        quant("2", 2, 4)
+        quant("h", 1, 2)
         copy(scopy, "g", 2)
+        quant("g", 1, 2)
+        lps[1] = stage2_mm(1)
         copy(scopy, "h", 3)
         copy(scopy, "g", 3)
+        logits_add(lps[0], 0)
         quant("h", 2, 3)
-        logits_max(lps[0], 0)
+        logits_max(0)
         exps(0)
         quant("g", 2, 3)
         lps[2] = stage2_mm(2)
+        logits_add(lps[1], 1)
         quant("h", 3, 4)
-        logits_max(lps[1], 1)
+        logits_max(1)
         exps(1)
         quant("g", 3, 4)
-        lps[3] = stage2_mm(3)
+        lps[3] = stage2_mm(3, warm=1)
         for pair in range(2, PAIRS):
-            logits_max(lps[pair], pair)
+            logits_add(lps[pair], pair)
+            logits_max(pair)
             exps(pair)
         nc.scalar.activation(out=lse[:], in_=ssum[:], func=ACT.Ln)
         out_rows = out.rearrange("(p i) c -> p (i c)", i=TILES)

@@ -153,14 +153,18 @@ def tile_gin_pc_kernel(tc, u1, W2_1, b2_1, h, h1, W_out, b_out, out):
                     out=dst[:, :, t], in_=hp[:, t, :], func=ACT.Identity, bias=b2_raw[:, t : t + 1], scale=1.0
                 )
 
-        def stage2_mm(pair, warm=0):
+        def stage2_mm(pair, warm=0, split=False):
             lp = psum.tile([P, 2, CLASSES], F32, tag="bank")
             keep_warm(lp[:, 0, :], warm)
+            lp_of = [lp, lp]
+            if split:
+                second = psum.tile([P, 2, CLASSES], F32, tag="bank")
+                lp_of = [lp, second]
             for s in range(2):
                 i = 2 * pair + s
                 for g, (c, sc) in enumerate(((h_c, h_s), (h1_c, h1_s), (h2_c, h2_s))):
                     nc.tensor.matmul_mx(
-                        out=lp[:, s, :],
+                        out=lp_of[s][:, s, :],
                         lhsT=c[:, i * P : (i + 1) * P].bitcast(FP8X4),
                         lhsT_scale=sc[:, i * P : (i + 1) * P],
                         rhs=wo_c[:, g * CLASSES : (g + 1) * CLASSES].bitcast(FP8X4),
@@ -168,7 +172,7 @@ def tile_gin_pc_kernel(tc, u1, W2_1, b2_1, h, h1, W_out, b_out, out):
                         start=(g == 0),
                         stop=(g == 2),
                     )
-            return lp
+            return lp_of if split else lp
 
         def logits_add(lp, pair):
             zp = z[:, 2 * pair * CLASSES : (2 * pair + 2) * CLASSES].rearrange("p (s c) -> p s c", s=2)
@@ -180,6 +184,16 @@ def tile_gin_pc_kernel(tc, u1, W2_1, b2_1, h, h1, W_out, b_out, out):
             zp = z[:, 2 * pair * CLASSES : (2 * pair + 2) * CLASSES].rearrange("p (s c) -> p s c", s=2)
             nc.vector.tensor_reduce(
                 out=negm[:, 2 * pair : 2 * pair + 2], in_=zp, axis=AX.X, op=ALU.max, negate=True
+            )
+
+        def logits_add_tile(lp, i, s):
+            nc.vector.tensor_tensor(
+                out=z[:, i * CLASSES : (i + 1) * CLASSES], in0=lp[:, s, :], in1=bo[:], op=ALU.add
+            )
+
+        def logits_max_tile(i):
+            nc.vector.tensor_reduce(
+                out=negm[:, i : i + 1], in_=z[:, i * CLASSES : (i + 1) * CLASSES], axis=AX.X, op=ALU.max, negate=True
             )
 
         def exps(pair):
@@ -292,11 +306,15 @@ def tile_gin_pc_kernel(tc, u1, W2_1, b2_1, h, h1, W_out, b_out, out):
         logits_max(1)
         exps(1)
         quant("g", 3, 4)
-        lps[3] = stage2_mm(3, warm=1)
-        for pair in range(2, PAIRS):
-            logits_add(lps[pair], pair)
-            logits_max(pair)
-            exps(pair)
+        lps[3] = stage2_mm(3, warm=1, split=True)
+        logits_add(lps[2], 2)
+        logits_max(2)
+        exps(2)
+        for s in range(2):
+            logits_add_tile(lps[3][s], 6 + s, s)
+        for s in range(2):
+            logits_max_tile(6 + s)
+        exps(3)
         nc.scalar.activation(out=lse[:], in_=ssum[:], func=ACT.Ln)
         out_rows = out.rearrange("(p i) c -> p (i c)", i=TILES)
         for pair in range(PAIRS):

@@ -88,18 +88,15 @@ def tile_gin_pc_kernel(tc, u1, W2_1, b2_1, h, h1, W_out, b_out, out):
         u1_g = keep.tile([P, TILES * HID], BF16, align_bytes=64)
         u1_c = keep.tile([P, NODES], U32, align_bytes=64)
         u1_s = keep.tile([P, NODES], U8, align_bytes=64)
-        h_g = keep.tile([P, TILES * HID], BF16, align_bytes=64)
-        h_c = keep.tile([P, NODES], U32, align_bytes=64)
-        h_s = keep.tile([P, NODES], U8, align_bytes=64)
-        h1_g = keep.tile([P, TILES * HID], BF16, align_bytes=64)
-        h1_c = keep.tile([P, NODES], U32, align_bytes=64)
-        h1_s = keep.tile([P, NODES], U8, align_bytes=64)
+        hg_g = keep.tile([P, 2 * TILES * HID], BF16, align_bytes=64)
+        hg_c = keep.tile([P, 2 * NODES], U32, align_bytes=64)
+        hg_s = keep.tile([P, 2 * NODES], U8, align_bytes=64)
         h2_g = keep.tile([P, TILES * HID], BF16, align_bytes=64)
         h2_c = keep.tile([P, NODES], U32, align_bytes=64)
         h2_s = keep.tile([P, NODES], U8, align_bytes=64)
         bo = keep.tile([P, CLASSES], F32)
         z = keep.tile([P, TILES * CLASSES], F32)
-        junk = keep.tile([P, CLASSES], F32)
+        junk = keep.tile([P, TILES * CLASSES], F32)
         negm = keep.tile([P, TILES], F32)
         ssum = keep.tile([P, TILES], F32)
         lse = keep.tile([P, TILES], F32)
@@ -117,8 +114,8 @@ def tile_gin_pc_kernel(tc, u1, W2_1, b2_1, h, h1, W_out, b_out, out):
                     nc.tensor.transpose(tp[:, s, u, :], words[:, col + u : col + WORDS : 2], ident[:])
             return tp
 
-        def copy_out(engine_copy, tp, g, pair):
-            dst = g[:].bitcast(F32)[:, 2 * pair * WORDS : (2 * pair + 2) * WORDS]
+        def copy_out(engine_copy, tp, g, slot):
+            dst = g[:].bitcast(F32)[:, 2 * slot * WORDS : (2 * slot + 2) * WORDS]
             engine_copy(
                 out=dst.rearrange("p (s n u) -> p s n u", s=2, u=2),
                 in_=tp[:].rearrange("p s u n -> p s n u"),
@@ -153,26 +150,27 @@ def tile_gin_pc_kernel(tc, u1, W2_1, b2_1, h, h1, W_out, b_out, out):
                     out=dst[:, :, t], in_=hp[:, t, :], func=ACT.Identity, bias=b2_raw[:, t : t + 1], scale=1.0
                 )
 
-        def stage2_mm(pair, warm=0, split=False):
+        def stage2_mm(pair, warm=0):
             lp = psum.tile([P, 2, CLASSES], F32, tag="bank")
             keep_warm(lp[:, 0, :], warm)
-            lp_of = [lp, lp]
-            if split:
-                second = psum.tile([P, 2, CLASSES], F32, tag="bank")
-                lp_of = [lp, second]
             for s in range(2):
                 i = 2 * pair + s
-                for g, (c, sc) in enumerate(((h_c, h_s), (h1_c, h1_s), (h2_c, h2_s))):
+                operands = (
+                    (hg_c, hg_s, 4 * pair + s),
+                    (hg_c, hg_s, 4 * pair + 2 + s),
+                    (h2_c, h2_s, i),
+                )
+                for g, (c, sc, k) in enumerate(operands):
                     nc.tensor.matmul_mx(
-                        out=lp_of[s][:, s, :],
-                        lhsT=c[:, i * P : (i + 1) * P].bitcast(FP8X4),
-                        lhsT_scale=sc[:, i * P : (i + 1) * P],
+                        out=lp[:, s, :],
+                        lhsT=c[:, k * P : (k + 1) * P].bitcast(FP8X4),
+                        lhsT_scale=sc[:, k * P : (k + 1) * P],
                         rhs=wo_c[:, g * CLASSES : (g + 1) * CLASSES].bitcast(FP8X4),
                         rhs_scale=wo_s[:, g * CLASSES : (g + 1) * CLASSES],
                         start=(g == 0),
                         stop=(g == 2),
                     )
-            return lp_of if split else lp
+            return lp
 
         def logits_add(lp, pair):
             zp = z[:, 2 * pair * CLASSES : (2 * pair + 2) * CLASSES].rearrange("p (s c) -> p s c", s=2)
@@ -180,26 +178,14 @@ def tile_gin_pc_kernel(tc, u1, W2_1, b2_1, h, h1, W_out, b_out, out):
                 out=zp, in0=lp[:], in1=bo[:].unsqueeze(1).to_broadcast([P, 2, CLASSES]), op=ALU.add
             )
 
-        def logits_max(pair):
-            zp = z[:, 2 * pair * CLASSES : (2 * pair + 2) * CLASSES].rearrange("p (s c) -> p s c", s=2)
-            nc.vector.tensor_reduce(
-                out=negm[:, 2 * pair : 2 * pair + 2], in_=zp, axis=AX.X, op=ALU.max, negate=True
-            )
-
-        def logits_add_tile(lp, i, s):
-            nc.vector.tensor_tensor(
-                out=z[:, i * CLASSES : (i + 1) * CLASSES], in0=lp[:, s, :], in1=bo[:], op=ALU.add
-            )
-
-        def logits_max_tile(i):
-            nc.vector.tensor_reduce(
-                out=negm[:, i : i + 1], in_=z[:, i * CLASSES : (i + 1) * CLASSES], axis=AX.X, op=ALU.max, negate=True
-            )
+        def logits_max(lo, hi):
+            rows = z[:, lo * CLASSES : hi * CLASSES].rearrange("p (i c) -> p i c", i=hi - lo)
+            nc.vector.tensor_reduce(out=negm[:, lo:hi], in_=rows, axis=AX.X, op=ALU.max, negate=True)
 
         def exps(pair):
             for i in (2 * pair, 2 * pair + 1):
                 nc.scalar.activation(
-                    out=junk[:],
+                    out=junk[:, i * CLASSES : (i + 1) * CLASSES],
                     in_=z[:, i * CLASSES : (i + 1) * CLASSES],
                     func=ACT.Exp,
                     bias=negm[:, i : i + 1],
@@ -233,11 +219,17 @@ def tile_gin_pc_kernel(tc, u1, W2_1, b2_1, h, h1, W_out, b_out, out):
             tp[(name, pair)] = transposes({"u": u1_sb, "h": h_sb, "g": h1_sb}[name], pair, warm)
 
         def copy(engine_copy, name, pair):
-            copy_out(engine_copy, tp[(name, pair)], {"u": u1_g, "h": h_g, "g": h1_g}[name], pair)
+            g, slot = {"u": (u1_g, pair), "h": (hg_g, 2 * pair), "g": (hg_g, 2 * pair + 1)}[name]
+            copy_out(engine_copy, tp[(name, pair)], g, slot)
 
-        def quant(name, lo_pair, hi_pair):
-            g, c, s = {"u": (u1_g, u1_c, u1_s), "h": (h_g, h_c, h_s), "g": (h1_g, h1_c, h1_s), "2": (h2_g, h2_c, h2_s)}[name]
-            quantise(g, c, s, 2 * lo_pair * P, 2 * hi_pair * P)
+        def quant_u1(lo_pair, hi_pair):
+            quantise(u1_g, u1_c, u1_s, 2 * lo_pair * P, 2 * hi_pair * P)
+
+        def quant_hg(pair):
+            quantise(hg_g, hg_c, hg_s, 4 * pair * P, (4 * pair + 4) * P)
+
+        def quant_h2(lo_pair, hi_pair):
+            quantise(h2_g, h2_c, h2_s, 2 * lo_pair * P, 2 * hi_pair * P)
 
         trans("u", 0)
         trans("u", 1)
@@ -246,9 +238,9 @@ def tile_gin_pc_kernel(tc, u1, W2_1, b2_1, h, h1, W_out, b_out, out):
         trans("u", 3)
         copy(scopy, "u", 0)
         copy(vcopy, "u", 1)
-        quant("u", 0, 1)
+        quant_u1(0, 1)
         copy(scopy, "u", 2)
-        quant("u", 1, 2)
+        quant_u1(1, 2)
         copy(scopy, "u", 3)
         regroup_wo(0)
         regroup_wo(1)
@@ -258,7 +250,7 @@ def tile_gin_pc_kernel(tc, u1, W2_1, b2_1, h, h1, W_out, b_out, out):
         trans("h", 1)
         stage1_out(hps[0], 0)
         stage1_out_scalar(hps[1], 1)
-        quant("u", 2, 4)
+        quant_u1(2, 4)
         stage1_out(hps[2], 2)
         stage1_out(hps[3], 3)
         copy(scopy, "h", 0)
@@ -270,50 +262,44 @@ def tile_gin_pc_kernel(tc, u1, W2_1, b2_1, h, h1, W_out, b_out, out):
         trans("g", 0)
         trans("g", 1)
         trans("h", 2)
+        regroup_wo(2)
         stage1_out(hps[4], 4)
         stage1_out_scalar(hps[5], 5)
         nc.scalar.copy(out=bo[:], in_=bp[:])
         stage1_out(hps[6], 6)
         stage1_out(hps[7], 7)
-        regroup_wo(2)
-        quant("2", 0, 2)
         trans("g", 2, warm=1)
         trans("h", 3)
         trans("g", 3)
+        quant_h2(0, 2)
         copy(scopy, "g", 0)
         copy(scopy, "g", 1)
         quantise(wo_g, wo_c, wo_s, 0, 2 * CLASSES)
-        quant("h", 0, 1)
-        quant("g", 0, 1)
+        quant_hg(0)
         quantise(wo_g, wo_c, wo_s, 2 * CLASSES, 3 * CLASSES)
+
         lps[0] = stage2_mm(0)
         copy(scopy, "h", 2)
-        quant("2", 2, 4)
-        quant("h", 1, 2)
+        quant_h2(2, 4)
+        quant_hg(1)
         copy(scopy, "g", 2)
-        quant("g", 1, 2)
         lps[1] = stage2_mm(1)
         copy(scopy, "h", 3)
         copy(scopy, "g", 3)
         logits_add(lps[0], 0)
-        quant("h", 2, 3)
-        logits_max(0)
-        exps(0)
-        quant("g", 2, 3)
+        quant_hg(2)
         lps[2] = stage2_mm(2)
         logits_add(lps[1], 1)
-        quant("h", 3, 4)
-        logits_max(1)
+        quant_hg(3)
+        lps[3] = stage2_mm(3)
+        logits_max(0, 4)
+        exps(0)
         exps(1)
-        quant("g", 3, 4)
-        lps[3] = stage2_mm(3, warm=1, split=True)
         logits_add(lps[2], 2)
-        logits_max(2)
+        logits_add(lps[3], 3)
+        logits_max(4, 6)
+        logits_max(6, 8)
         exps(2)
-        for s in range(2):
-            logits_add_tile(lps[3][s], 6 + s, s)
-        for s in range(2):
-            logits_max_tile(6 + s)
         exps(3)
         nc.scalar.activation(out=lse[:], in_=ssum[:], func=ACT.Ln)
         out_rows = out.rearrange("(p i) c -> p (i c)", i=TILES)

from contextlib import ExitStack

import concourse.mybir as mybir
from concourse.masks import make_identity

F32 = mybir.dt.float32
BF16 = mybir.dt.bfloat16
U32 = mybir.dt.uint32
U8 = mybir.dt.uint8
FP8X4 = mybir.dt.float8_e4m3fn_x4
ALU = mybir.AluOpType
ACT = mybir.ActivationFunctionType
AX = mybir.AxisListType

P = 128
NODES = 1024
HID = 512
CLASSES = 256
TILES = NODES // P
PAIRS = TILES // 2
WORDS = HID // 2
FLOPS = 2 * NODES * HID * HID + 2 * NODES * 3 * HID * CLASSES


def tile_gin_pc_kernel(tc, u1, W2_1, b2_1, h, h1, W_out, b_out, out):
    nc = tc.nc
    with ExitStack() as ctx:
        keep = ctx.enter_context(tc.tile_pool(name="keep", bufs=1))
        psum = ctx.enter_context(tc.psum_pool(name="psum", bufs=8))
        ctx.enter_context(tc.manual_schedule())

        ident = keep.tile([P, P], F32)
        make_identity(nc, ident[:])
        ones = keep.tile([P, P], BF16)
        nc.gpsimd.memset(ones[:], 1.0)
        bo_rows = keep.tile([P, CLASSES], BF16)
        nc.vector.memset(bo_rows[:], 0.0)
        warm_rhs = keep.tile([P, CLASSES], F32)
        nc.vector.memset(warm_rhs[:], 0.0)
        warm_out = psum.tile([P, CLASSES], F32, tag="bank")

        def keep_warm(out, times):
            for rep in range(times):
                nc.tensor.matmul(out=out, lhsT=ident[:], rhs=warm_rhs[:], start=True, stop=True)

        keep_warm(warm_out[:], 4)

        w2_raw = keep.tile([P, 4 * HID], BF16)
        u1_sb = keep.tile([P, TILES * HID], BF16)
        h_sb = keep.tile([P, TILES * HID], BF16)
        h1_sb = keep.tile([P, TILES * HID], BF16)
        wo_raw = keep.tile([P, 12 * CLASSES], BF16)
        b2_raw = keep.tile([P, 4], BF16)

        def load_tiles(x_sb, x, lo, hi):
            cols = slice(lo * HID, hi * HID)
            nc.sync.dma_start(out=x_sb[:, cols], in_=x.rearrange("(p i) k -> p (i k)", i=TILES)[:, cols])

        nc.scalar.dma_start(out=b2_raw[:], in_=b2_1.rearrange("(p t) -> p t", t=4))
        nc.scalar.dma_start(out=bo_rows[0:1, :], in_=b_out.rearrange("(o c) -> o c", o=1))
        nc.sync.dma_start(
            out=w2_raw[:],
            in_=W2_1.rearrange("(q t) c -> q (t c)", t=4),
        )
        load_tiles(u1_sb, u1, 0, 2)
        load_tiles(u1_sb, u1, 2, 4)
        load_tiles(u1_sb, u1, 4, 6)
        load_tiles(u1_sb, u1, 6, 8)
        nc.sync.dma_start(
            out=wo_raw[:, 0 : 8 * CLASSES].rearrange("q (g x) -> q g x", g=2),
            in_=W_out[0 : 2 * HID, :].rearrange("(g q t) c -> q g (t c)", g=2, t=4),
        )
        load_tiles(h_sb, h, 0, 4)
        load_tiles(h1_sb, h1, 0, 4)
        nc.sync.dma_start(
            out=wo_raw[:, 8 * CLASSES : 12 * CLASSES],
            in_=W_out[2 * HID : 3 * HID, :].rearrange("(q t) c -> q (t c)", t=4),
        )
        load_tiles(h_sb, h, 4, 8)
        load_tiles(h1_sb, h1, 4, 8)

        w2_g = keep.tile([P, 4 * HID], BF16, align_bytes=64)
        w2_c = keep.tile([P, HID], U32, align_bytes=64)
        w2_s = keep.tile([P, HID], U8, align_bytes=64)
        wo_g = keep.tile([P, 12 * CLASSES], BF16, align_bytes=64)
        wo_c = keep.tile([P, 3 * CLASSES], U32, align_bytes=64)
        wo_s = keep.tile([P, 3 * CLASSES], U8, align_bytes=64)
        u1_g = keep.tile([P, TILES * HID], BF16, align_bytes=64)
        u1_c = keep.tile([P, NODES], U32, align_bytes=64)
        u1_s = keep.tile([P, NODES], U8, align_bytes=64)
        hg_g = keep.tile([P, 2 * TILES * HID], BF16, align_bytes=64)
        hg_c = keep.tile([P, 2 * NODES], U32, align_bytes=64)
        hg_s = keep.tile([P, 2 * NODES], U8, align_bytes=64)
        h2_g = keep.tile([P, TILES * HID], BF16, align_bytes=64)
        h2_c = keep.tile([P, NODES], U32, align_bytes=64)
        h2_s = keep.tile([P, NODES], U8, align_bytes=64)
        bo = keep.tile([P, CLASSES], F32)
        z = keep.tile([P, TILES * CLASSES], F32)
        junk = keep.tile([P, TILES * CLASSES], F32)
        negm = keep.tile([P, TILES], F32)
        ssum = keep.tile([P, TILES], F32)
        lse = keep.tile([P, TILES], F32)

        def quantise(g, c, s, lo, hi):
            nc.vector.quantize_mx(out=c[:, lo:hi].bitcast(FP8X4), scales=s[:, lo:hi], in_=g[:, 4 * lo : 4 * hi])

        def transposes(x_sb, pair, warm):
            tp = psum.tile([P, 2, 2, P], F32, tag="bank")
            keep_warm(tp[:, 0, :, :], warm)
            words = x_sb[:].bitcast(F32)
            for s in range(2):
                for u in range(2):
                    col = (2 * pair + s) * WORDS
                    nc.tensor.transpose(tp[:, s, u, :], words[:, col + u : col + WORDS : 2], ident[:])
            return tp

        def copy_out(engine_copy, tp, g, slot):
            dst = g[:].bitcast(F32)[:, 2 * slot * WORDS : (2 * slot + 2) * WORDS]
            engine_copy(
                out=dst.rearrange("p (s n u) -> p s n u", s=2, u=2),
                in_=tp[:].rearrange("p s u n -> p s n u"),
            )

        def stage1_mm(i):
            hp = psum.tile([P, 4, P], F32, tag="bank")
            for t in range(4):
                nc.tensor.matmul_mx(
                    out=hp[:, t, :],
                    lhsT=w2_c[:, t * P : (t + 1) * P].bitcast(FP8X4),
                    lhsT_scale=w2_s[:, t * P : (t + 1) * P],
                    rhs=u1_c[:, i * P : (i + 1) * P].bitcast(FP8X4),
                    rhs_scale=u1_s[:, i * P : (i + 1) * P],
                    start=True,
                    stop=True,
                )
            return hp

        def stage1_out(hp, i):
            nc.vector.tensor_tensor(
                out=h2_g[:, i * HID : (i + 1) * HID].rearrange("p (n t) -> p n t", t=4),
                in0=hp[:].rearrange("p t n -> p n t"),
                in1=b2_raw[:].unsqueeze(1).to_broadcast([P, P, 4]),
                op=ALU.add,
            )

        def stage1_out_scalar(hp, i):
            dst = h2_g[:, i * HID : (i + 1) * HID].rearrange("p (n t) -> p n t", t=4)
            for t in range(4):
                nc.scalar.activation(
                    out=dst[:, :, t], in_=hp[:, t, :], func=ACT.Identity, bias=b2_raw[:, t : t + 1], scale=1.0
                )

        def stage2_mm(pair, warm=0):
            lp = psum.tile([P, 2, CLASSES], F32, tag="bank")
            keep_warm(lp[:, 0, :], warm)
            for s in range(2):
                i = 2 * pair + s
                operands = (
                    (hg_c, hg_s, 4 * pair + s),
                    (hg_c, hg_s, 4 * pair + 2 + s),
                    (h2_c, h2_s, i),
                )
                for g, (c, sc, k) in enumerate(operands):
                    nc.tensor.matmul_mx(
                        out=lp[:, s, :],
                        lhsT=c[:, k * P : (k + 1) * P].bitcast(FP8X4),
                        lhsT_scale=sc[:, k * P : (k + 1) * P],
                        rhs=wo_c[:, g * CLASSES : (g + 1) * CLASSES].bitcast(FP8X4),
                        rhs_scale=wo_s[:, g * CLASSES : (g + 1) * CLASSES],
                        start=(g == 0),
                        stop=(g == 2),
                    )
            return lp

        def logits_add(lp, pair):
            zp = z[:, 2 * pair * CLASSES : (2 * pair + 2) * CLASSES].rearrange("p (s c) -> p s c", s=2)
            nc.vector.tensor_tensor(
                out=zp, in0=lp[:], in1=bo[:].unsqueeze(1).to_broadcast([P, 2, CLASSES]), op=ALU.add
            )

        def logits_max(lo, hi):
            rows = z[:, lo * CLASSES : hi * CLASSES].rearrange("p (i c) -> p i c", i=hi - lo)
            nc.vector.tensor_reduce(out=negm[:, lo:hi], in_=rows, axis=AX.X, op=ALU.max, negate=True)

        def exps(pair):
            for i in (2 * pair, 2 * pair + 1):
                nc.scalar.activation(
                    out=junk[:, i * CLASSES : (i + 1) * CLASSES],
                    in_=z[:, i * CLASSES : (i + 1) * CLASSES],
                    func=ACT.Exp,
                    bias=negm[:, i : i + 1],
                    scale=1.0,
                    accum_out=ssum[:, i : i + 1],
                )

        w2_dst = w2_g[:].rearrange("p (t2 p2 t) -> p t2 p2 t", t2=4, t=4)
        w2_src = w2_raw[:].rearrange("p (t p2 t2) -> p t2 p2 t", t=4, t2=4)
        nc.vector.tensor_copy(out=w2_dst[:, 0:2], in_=w2_src[:, 0:2])
        nc.scalar.copy(out=w2_dst[:, 2:4], in_=w2_src[:, 2:4])

        def regroup_wo(g):
            cols = slice(g * 4 * CLASSES, (g + 1) * 4 * CLASSES)
            nc.gpsimd.tensor_scalar(
                out=wo_g[:, cols].rearrange("p (c t) -> p c t", t=4),
                in0=wo_raw[:, cols].rearrange("p (t c) -> p c t", t=4),
                scalar1=1.0,
                scalar2=0.0,
                op0=ALU.mult,
                op1=ALU.add,
            )

        scopy = nc.scalar.copy
        vcopy = nc.vector.tensor_copy
        tp = {}
        hps = {}
        lps = {}

        def trans(name, pair, warm=0):
            tp[(name, pair)] = transposes({"u": u1_sb, "h": h_sb, "g": h1_sb}[name], pair, warm)

        def copy(engine_copy, name, pair):
            g, slot = {"u": (u1_g, pair), "h": (hg_g, 2 * pair), "g": (hg_g, 2 * pair + 1)}[name]
            copy_out(engine_copy, tp[(name, pair)], g, slot)

        def quant_u1(lo_pair, hi_pair):
            quantise(u1_g, u1_c, u1_s, 2 * lo_pair * P, 2 * hi_pair * P)

        def quant_hg(pair):
            quantise(hg_g, hg_c, hg_s, 4 * pair * P, (4 * pair + 4) * P)

        def quant_h2(lo_pair, hi_pair):
            quantise(h2_g, h2_c, h2_s, 2 * lo_pair * P, 2 * hi_pair * P)

        trans("u", 0)
        trans("u", 1)
        quantise(w2_g, w2_c, w2_s, 0, HID)
        trans("u", 2, warm=1)
        trans("u", 3)
        copy(scopy, "u", 0)
        copy(vcopy, "u", 1)
        quant_u1(0, 1)
        copy(scopy, "u", 2)
        quant_u1(1, 2)
        copy(scopy, "u", 3)
        regroup_wo(0)
        regroup_wo(1)
        for i in range(4):
            hps[i] = stage1_mm(i)
        trans("h", 0)
        trans("h", 1)
        stage1_out(hps[0], 0)
        stage1_out_scalar(hps[1], 1)
        quant_u1(2, 4)
        stage1_out(hps[2], 2)
        stage1_out(hps[3], 3)
        copy(scopy, "h", 0)
        for i in range(4, 8):
            hps[i] = stage1_mm(i)
        copy(scopy, "h", 1)
        bp = psum.tile([P, CLASSES], F32, tag="bank")
        nc.tensor.matmul(out=bp[:], lhsT=ones[:], rhs=bo_rows[:], start=True, stop=True)
        trans("g", 0)
        trans("g", 1)
        trans("h", 2)
        regroup_wo(2)
        stage1_out(hps[4], 4)
        stage1_out_scalar(hps[5], 5)
        nc.scalar.copy(out=bo[:], in_=bp[:])
        stage1_out(hps[6], 6)
        stage1_out(hps[7], 7)
        trans("g", 2, warm=1)
        trans("h", 3)
        trans("g", 3)
        quant_h2(0, 2)
        copy(scopy, "g", 0)
        copy(scopy, "g", 1)
        quantise(wo_g, wo_c, wo_s, 0, 2 * CLASSES)
        quant_hg(0)
        quantise(wo_g, wo_c, wo_s, 2 * CLASSES, 3 * CLASSES)

        lps[0] = stage2_mm(0)
        copy(scopy, "h", 2)
        quant_h2(2, 4)
        quant_hg(1)
        copy(scopy, "g", 2)
        lps[1] = stage2_mm(1)
        copy(scopy, "h", 3)
        copy(scopy, "g", 3)
        logits_add(lps[0], 0)
        quant_hg(2)
        lps[2] = stage2_mm(2)
        logits_add(lps[1], 1)
        quant_hg(3)
        lps[3] = stage2_mm(3)
        logits_max(0, 4)
        exps(0)
        exps(1)
        logits_add(lps[2], 2)
        logits_add(lps[3], 3)
        logits_max(4, 6)
        logits_max(6, 8)
        exps(2)
        exps(3)
        nc.scalar.activation(out=lse[:], in_=ssum[:], func=ACT.Ln)
        out_rows = out.rearrange("(p i) c -> p (i c)", i=TILES)
        for pair in range(PAIRS):
            for i in (2 * pair, 2 * pair + 1):
                zi = z[:, i * CLASSES : (i + 1) * CLASSES]
                nc.vector.tensor_scalar(
                    out=zi,
                    in0=zi,
                    scalar1=negm[:, i : i + 1],
                    scalar2=lse[:, i : i + 1],
                    op0=ALU.add,
                    op1=ALU.subtract,
                )
            cols = slice(2 * pair * CLASSES, (2 * pair + 2) * CLASSES)
            nc.sync.dma_start(out=out_rows[:, cols], in_=z[:, cols])
